import numpy as np
import ml_dtypes


def mxq(x, axis, fmt="e4m3"):
    dtype, down = {"e4m3": (ml_dtypes.float8_e4m3fn, 7), "e5m2": (ml_dtypes.float8_e5m2, 14)}[fmt]
    v = np.moveaxis(np.asarray(x, np.float32).astype(ml_dtypes.bfloat16).astype(np.float64), axis, -1)
    blocks = v.reshape(v.shape[:-1] + (-1, 32))
    amax = np.abs(blocks).max(-1, keepdims=True)
    byte = np.maximum(np.where(amax > 0, np.frexp(amax)[1] - 1 + 127, 0) - down, 1)
    scale = np.exp2(byte - 127.0)
    codes = (blocks / scale).astype(np.float32).astype(dtype).astype(np.float64)
    return np.moveaxis((codes * scale).reshape(v.shape), -1, axis)


WIDE = False


def mx_kscale(k):
    if not WIDE:
        return np.ones(k)
    levels = np.array([10, -10, 5, -5, 0])
    if k % 512:
        return np.exp2(np.random.permutation(np.resize(levels, k // 32))).repeat(32)
    a = np.empty((k // 512, 16))
    for p in range(k // 512):
        a[p, :8] = np.random.permutation(np.resize(levels, 8))
        for g in range(8):
            far = levels[np.abs(levels - a[p, g]) >= 10]
            a[p, g + 8] = far[np.random.randint(len(far))]
    return np.exp2(a.ravel()).repeat(32)


BF16 = ml_dtypes.bfloat16


def bf(x):
    return np.asarray(x, np.float32).astype(BF16)


def f64(x):
    return np.asarray(x).astype(np.float64)


B, L, N, RS, D, H, A, F = 4, 4, 128, 16, 512, 8, 64, 2048
S = L * (N + RS)
EPS = 1e-05


def rmsnorm(x, w):
    return x / np.sqrt(np.mean(x * x, -1, keepdims=True) + EPS) * w


def silu(v):
    return v / (1.0 + np.exp(-v))


def setup_inputs():
    s, t = mx_kscale(D), mx_kscale(D)
    return {'o_attn': bf(np.random.standard_normal((B, S, D)) * 0.14 * s),
            'xm': bf(np.random.standard_normal((B, S, D))),
            'attn_o_w': bf(np.random.standard_normal((D, D)) * 3.0 / np.sqrt(D) / s[:, None]),
            'ffn_norm_w': bf((1.0 + 0.1 * np.random.standard_normal(D)) * t),
            'ffn_up_w': bf(np.random.standard_normal((D, 2 * F)) / np.sqrt(D) / t[:, None])}


def reference(o_attn, xm, attn_o_w, ffn_norm_w, ffn_up_w):
    x2 = (mxq(f64(o_attn), 2, 'e4m3') @ mxq(f64(attn_o_w), 0, 'e4m3')) + f64(xm)
    xn2 = rmsnorm(x2, f64(ffn_norm_w))
    u1, u2 = np.split(mxq(xn2, 2, 'e4m3') @ mxq(f64(ffn_up_w), 0, 'e4m3'), 2, axis=-1)
    return x2, silu(u1) * u2

@@ -1,0 +1,235 @@
+from contextlib import ExitStack
+
+import concourse.mybir as mybir
+from concourse.masks import make_identity
+
+F32 = mybir.dt.float32
+BF16 = mybir.dt.bfloat16
+U32 = mybir.dt.uint32
+U8 = mybir.dt.uint8
+FP8X4 = mybir.dt.float8_e4m3fn_x4
+ACT = mybir.ActivationFunctionType
+ALU = mybir.AluOpType
+
+P = 128
+PACK = 4
+D = P * PACK
+TOKENS = 4 * 576
+TILES = TOKENS // P
+PAIR = 2
+PAIRS = TILES // PAIR
+F = 2048
+N_PASS = 512
+CHUNKS = F // N_PASS
+LEAD = 6
+EPS = 1e-5
+
+FLOPS = 2 * TOKENS * D * (D + 2 * F)
+
+
+def tile_model_pb_kernel(tc, o_attn, xm, attn_o_w, ffn_norm_w, ffn_up_w, out_0, out_1):
+    nc = tc.nc
+
+    o_rows = o_attn.flatten_outer_dims().rearrange("(p j) d -> p j d", j=TILES)
+    xm_rows = xm.flatten_outer_dims().rearrange("(p j) d -> p j d", j=TILES)
+    x2_rows = out_0.flatten_outer_dims().rearrange("(p j) d -> p j d", j=TILES)
+    h_rows = out_1.flatten_outer_dims().rearrange("(p j) f -> p j f", j=TILES)
+
+    with ExitStack() as ctx:
+        ctx.enter_context(tc.manual_schedule())
+        loads = ctx.enter_context(tc.tile_pool(name="loads", bufs=1))
+        consts = ctx.enter_context(tc.tile_pool(name="consts", bufs=1))
+        weights = ctx.enter_context(tc.tile_pool(name="weights", bufs=1))
+        regroup = ctx.enter_context(tc.tile_pool(name="regroup", bufs=4))
+        stage = ctx.enter_context(tc.tile_pool(name="stage", bufs=4))
+        gated = ctx.enter_context(tc.tile_pool(name="gated", bufs=4))
+        results = ctx.enter_context(tc.tile_pool(name="results", bufs=3))
+        psum = ctx.enter_context(tc.psum_pool(name="psum", bufs=1))
+
+        gain_row = consts.tile([P, D], BF16)
+        nc.vector.memset(gain_row[:], 0.0)
+        nc.sync.dma_start(out=gain_row[0:1, :], in_=ffn_norm_w.unsqueeze(0))
+
+        o_sb = []
+        xm_sb = []
+
+        def load_pair(i):
+            tiles = slice(PAIR * i, PAIR * (i + 1))
+            o_sb.append(loads.tile([P, PAIR, D], BF16, name="o_sb%d" % i))
+            nc.sync.dma_start(out=o_sb[i][:], in_=o_rows[:, tiles, :])
+            xm_sb.append(loads.tile([P, PAIR, D], BF16, name="xm_sb%d" % i))
+            nc.sync.dma_start(out=xm_sb[i][:], in_=xm_rows[:, tiles, :])
+
+        load_pair(0)
+        wo_raw = loads.tile([P, PACK, D], BF16)
+        nc.sync.dma_start(out=wo_raw[:], in_=attn_o_w.rearrange("(p t) n -> p t n", t=PACK))
+        up_rows = ffn_up_w.rearrange("(p t) n -> p t n", t=PACK)
+        up_raw = [[], []]
+        for c in range(CHUNKS):
+            for half in range(2):
+                raw = loads.tile([P, PACK, N_PASS], BF16, name="up_raw%d_%d" % (half, c))
+                first = F * half + N_PASS * c
+                nc.sync.dma_start(out=raw[:], in_=up_rows[:, :, first : first + N_PASS])
+                up_raw[half].append(raw)
+            load_pair(c + 1)
+        for i in range(CHUNKS + 1, PAIRS):
+            load_pair(i)
+
+        ident_f32 = consts.tile([P, P], F32)
+        make_identity(nc, ident_f32[:])
+        ident_bf16 = consts.tile([P, P], BF16)
+        make_identity(nc, ident_bf16[:])
+        ones = consts.tile([P, P], BF16)
+        nc.vector.memset(ones[:], 1.0)
+        neg_half = consts.tile([P, 1], F32)
+        nc.vector.memset(neg_half[:], -0.5)
+
+        gain_ps = psum.tile([P, D], F32, tag="acc")
+        nc.tensor.matmul(out=gain_ps[:], lhsT=ones[:], rhs=gain_row[:], start=True, stop=True)
+        gain = consts.tile([P, D], F32)
+        nc.vector.tensor_copy(out=gain[:], in_=gain_ps[:])
+
+        def regroup_weight(copy_engine, raw):
+            grouped = regroup.tile([P, N_PASS, PACK], BF16, tag="grouped", align_bytes=64)
+            copy_engine(
+                out=grouped[:].rearrange("p (c i) t -> p c t i", i=4),
+                in_=raw[:].rearrange("p t (c i) -> p c t i", i=4),
+            )
+            return grouped
+
+        def quantise_weight(grouped, name):
+            codes = weights.tile([P, N_PASS], U32, name=name + "_codes", align_bytes=64)
+            scales = weights.tile([P, N_PASS], U8, name=name + "_scales", align_bytes=64)
+            nc.vector.quantize_mx(
+                out=codes[:].bitcast(FP8X4),
+                scales=scales[:],
+                in_=grouped[:].rearrange("p w t -> p (w t)"),
+            )
+            return codes, scales
+
+        wo_q = []
+        up_grouped = {}
+        up_q = {}
+
+        def prepare_weights(it):
+            if it == -LEAD:
+                wo_q.extend(quantise_weight(regroup_weight(nc.vector.tensor_copy, wo_raw), "wo"))
+            c = it + LEAD - 1
+            if 0 <= c < CHUNKS:
+                up_grouped[0, c] = regroup_weight(nc.vector.tensor_copy, up_raw[0][c])
+                up_grouped[1, c] = regroup_weight(nc.scalar.copy, up_raw[1][c])
+            if 0 <= c - 1 < CHUNKS:
+                for half in range(2):
+                    up_q[half, c - 1] = quantise_weight(up_grouped[half, c - 1], "up%d_%d" % (half, c - 1))
+
+        live = {}
+
+        def in_range(j):
+            return 0 <= j < TILES
+
+        def first_stage(it):
+            ja, jb, jc, je = it + 6, it + 5, it + 4, it + 2
+            if in_range(jb):
+                acc = psum.tile([P, D], F32, tag="acc")
+                nc.tensor.matmul_mx(
+                    out=acc[:],
+                    lhsT=live["o_codes", jb][:].bitcast(FP8X4),
+                    lhsT_scale=live["o_scales", jb][:],
+                    rhs=wo_q[0][:].bitcast(FP8X4),
+                    rhs_scale=wo_q[1][:],
+                    start=True,
+                    stop=True,
+                )
+            if in_range(ja):
+                words = o_sb[ja // PAIR][:].bitcast(F32)
+                oT = psum.tile([P, 2, P], F32)
+                for u in range(2):
+                    nc.tensor.transpose(oT[:, u, :], words[:, ja % PAIR, u : D // 2 : 2], ident_f32[:])
+            if in_range(je):
+                xnT = psum.tile([P, PACK, P], BF16)
+                for t in range(PACK):
+                    nc.tensor.transpose(xnT[:, t, :], live["xn", je][:, t, :], ident_bf16[:])
+
+            if in_range(ja):
+                o_grouped = stage.tile([P, P * PACK], BF16, align_bytes=64)
+                nc.vector.tensor_copy(
+                    out=o_grouped[:].bitcast(F32).rearrange("p (r u) -> p r u", u=2),
+                    in_=oT[:].rearrange("p u r -> p r u"),
+                )
+            if in_range(jb):
+                x2 = stage.tile([P, D], F32)
+                live["x2", jb] = x2
+                nc.vector.tensor_tensor(out=x2[:], in0=acc[:], in1=xm_sb[jb // PAIR][:, jb % PAIR, :], op=ALU.add)
+                nc.sync.dma_start(out=x2_rows[:, jb, :], in_=x2[:])
+            if in_range(jc):
+                squares = stage.tile([P, D], BF16)
+                mean_sq = stage.tile([P, 1], F32)
+                nc.scalar.activation(
+                    out=squares[:], in_=live["x2", jc][:], func=ACT.Square, scale=D**-0.5, accum_out=mean_sq[:]
+                )
+                shifted = stage.tile([P, 1], F32)
+                nc.gpsimd.tensor_scalar(
+                    out=shifted[:], in0=mean_sq[:], scalar1=1.0, scalar2=EPS, op0=ALU.mult, op1=ALU.add
+                )
+                rstd = stage.tile([P, 1], F32)
+                nc.gpsimd.tensor_tensor(out=rstd[:], in0=shifted[:], in1=neg_half[:], op=ALU.pow)
+                xn = stage.tile([P, PACK, P], BF16)
+                live["xn", jc] = xn
+                nc.gpsimd.tensor_scalar(
+                    out=xn[:],
+                    in0=live["x2_gain", jc][:].rearrange("p (m t) -> p t m", t=PACK),
+                    scalar1=rstd[:], scalar2=1.0, op0=ALU.mult, op1=ALU.mult
+                )
+            if in_range(jb):
+                x2_gain = stage.tile([P, D], F32)
+                live["x2_gain", jb] = x2_gain
+                nc.gpsimd.tensor_tensor(out=x2_gain[:], in0=x2[:], in1=gain[:], op=ALU.mult)
+            if in_range(ja):
+                o_codes = stage.tile([P, P], U32, align_bytes=64)
+                o_scales = stage.tile([P, P], U8, align_bytes=64)
+                live["o_codes", ja] = o_codes
+                live["o_scales", ja] = o_scales
+                nc.vector.quantize_mx(out=o_codes[:].bitcast(FP8X4), scales=o_scales[:], in_=o_grouped[:])
+            if in_range(je):
+                xn_grouped = stage.tile([P, P, PACK], BF16, align_bytes=64)
+                nc.scalar.copy(out=xn_grouped[:], in_=xnT[:].rearrange("p t r -> p r t"))
+                xn_codes = stage.tile([P, P], U32, align_bytes=64)
+                xn_scales = stage.tile([P, P], U8, align_bytes=64)
+                live["xn_codes", je] = xn_codes
+                live["xn_scales", je] = xn_scales
+                nc.vector.quantize_mx(
+                    out=xn_codes[:].bitcast(FP8X4),
+                    scales=xn_scales[:],
+                    in_=xn_grouped[:].rearrange("p r t -> p (r t)"),
+                )
+
+        def second_stage(j):
+            h = results.tile([P, F], F32)
+            for c in range(CHUNKS):
+                halves = []
+                for half in range(2):
+                    codes, scales = up_q[half, c]
+                    u_ps = psum.tile([P, N_PASS], F32, name="u%d" % half, bufs=2 + half)
+                    nc.tensor.matmul_mx(
+                        out=u_ps[:],
+                        lhsT=live["xn_codes", j][:].bitcast(FP8X4),
+                        lhsT_scale=live["xn_scales", j][:],
+                        rhs=codes[:].bitcast(FP8X4),
+                        rhs_scale=scales[:],
+                        start=True,
+                        stop=True,
+                    )
+                    halves.append(u_ps)
+                silu = gated.tile([P, N_PASS], F32)
+                nc.scalar.activation(out=silu[:], in_=halves[0][:], func=ACT.Silu)
+                nc.vector.tensor_tensor(
+                    out=h[:, N_PASS * c : N_PASS * (c + 1)], in0=halves[1][:], in1=silu[:], op=ALU.mult
+                )
+            nc.sync.dma_start(out=h_rows[:, j, :], in_=h[:])
+
+        for it in range(-LEAD, TILES):
+            if it < 0:
+                prepare_weights(it)
+            else:
+                second_stage(it)
+            first_stage(it)

@@ -48,54 +48,70 @@ def tile_model_pb_kernel(tc, o_attn, xm, attn_o_w, ffn_norm_w, ffn_up_w, out_0, 
 
         gain_row = consts.tile([P, D], BF16)
         nc.vector.memset(gain_row[:], 0.0)
-        nc.sync.dma_start(out=gain_row[0:1, :], in_=ffn_norm_w.unsqueeze(0))
-
-        o_sb = []
-        xm_sb = []
-
-        def load_pair(i):
-            tiles = slice(PAIR * i, PAIR * (i + 1))
-            o_sb.append(loads.tile([P, PAIR, D], BF16, name="o_sb%d" % i))
-            nc.sync.dma_start(out=o_sb[i][:], in_=o_rows[:, tiles, :])
-            xm_sb.append(loads.tile([P, PAIR, D], BF16, name="xm_sb%d" % i))
-            nc.sync.dma_start(out=xm_sb[i][:], in_=xm_rows[:, tiles, :])
-
-        load_pair(0)
-        wo_raw = loads.tile([P, PACK, D], BF16)
-        nc.sync.dma_start(out=wo_raw[:], in_=attn_o_w.rearrange("(p t) n -> p t n", t=PACK))
-        up_rows = ffn_up_w.rearrange("(p t) n -> p t n", t=PACK)
-        up_raw = [[], []]
-        for c in range(CHUNKS):
-            for half in range(2):
-                raw = loads.tile([P, PACK, N_PASS], BF16, name="up_raw%d_%d" % (half, c))
-                first = F * half + N_PASS * c
-                nc.sync.dma_start(out=raw[:], in_=up_rows[:, :, first : first + N_PASS])
-                up_raw[half].append(raw)
-            load_pair(c + 1)
-        for i in range(CHUNKS + 1, PAIRS):
-            load_pair(i)
-
+        dummy_in = consts.tile([P, 1], F32)
+        nc.vector.memset(dummy_in[:], 0.0)
+        dummy_out = consts.tile([P, 1], F32)
+        nc.scalar.activation(out=dummy_out[:], in_=dummy_in[:], func=ACT.Silu)
         ident_f32 = consts.tile([P, P], F32)
         make_identity(nc, ident_f32[:])
-        ident_bf16 = consts.tile([P, P], BF16)
-        make_identity(nc, ident_bf16[:])
         ones = consts.tile([P, P], BF16)
         nc.vector.memset(ones[:], 1.0)
         neg_half = consts.tile([P, 1], F32)
         nc.vector.memset(neg_half[:], -0.5)
 
+        o_sb = []
+        xm_sb = []
+
+        def load_o(i):
+            o_sb.append(loads.tile([P, PAIR, D], BF16, name="o_sb%d" % i))
+            nc.sync.dma_start(out=o_sb[i][:], in_=o_rows[:, PAIR * i : PAIR * (i + 1), :])
+
+        def load_xm(i):
+            xm_sb.append(loads.tile([P, PAIR, D], BF16, name="xm_sb%d" % i))
+            nc.sync.dma_start(out=xm_sb[i][:], in_=xm_rows[:, PAIR * i : PAIR * (i + 1), :])
+
+        wo_rows = attn_o_w.rearrange("(p t) n -> p t n", t=PACK)
+        up_rows = ffn_up_w.rearrange("(p t) n -> p t n", t=PACK)
+        wo_raw = loads.tile([P, PACK, D], BF16)
+        up_raw = [[], []]
+
+        def load_up(c):
+            for half in range(2):
+                raw = loads.tile([P, PACK, N_PASS], BF16, name="up_raw%d_%d" % (half, c))
+                first = F * half + N_PASS * c
+                nc.sync.dma_start(out=raw[:], in_=up_rows[:, :, first : first + N_PASS])
+                up_raw[half].append(raw)
+
+        load_o(0)
+        nc.sync.dma_start(out=gain_row[0:1, :], in_=ffn_norm_w.unsqueeze(0))
+        nc.sync.dma_start(out=wo_raw[:], in_=wo_rows)
+        load_up(0)
+        load_xm(0)
+        load_o(1)
+        load_up(1)
+        load_xm(1)
+        load_o(2)
+        load_up(2)
+        load_xm(2)
+        load_up(3)
+        for i in range(3, PAIRS):
+            load_o(i)
+            load_xm(i)
+
         gain_ps = psum.tile([P, D], F32, tag="acc")
         nc.tensor.matmul(out=gain_ps[:], lhsT=ones[:], rhs=gain_row[:], start=True, stop=True)
-        gain = consts.tile([P, D], F32)
-        nc.vector.tensor_copy(out=gain[:], in_=gain_ps[:])
+        gain = consts.tile([P, 2, P, 2], F32)
+        nc.vector.tensor_copy(out=gain[:], in_=gain_ps[:].rearrange("p (m u e) -> p u m e", u=2, e=2))
 
-        def regroup_weight(copy_engine, raw):
+        def new_grouped():
             grouped = regroup.tile([P, N_PASS, PACK], BF16, tag="grouped", align_bytes=64)
-            copy_engine(
-                out=grouped[:].rearrange("p (c i) t -> p c t i", i=4),
-                in_=raw[:].rearrange("p t (c i) -> p c t i", i=4),
-            )
             return grouped
+
+        def regroup_columns(copy_engine, grouped, raw, first, last):
+            copy_engine(
+                out=grouped[:, first:last, :].rearrange("p (c i) t -> p c t i", i=4),
+                in_=raw[:, :, first:last].rearrange("p t (c i) -> p c t i", i=4),
+            )
 
         def quantise_weight(grouped, name):
             codes = weights.tile([P, N_PASS], U32, name=name + "_codes", align_bytes=64)
@@ -108,16 +124,22 @@ def tile_model_pb_kernel(tc, o_attn, xm, attn_o_w, ffn_norm_w, ffn_up_w, out_0, 
             return codes, scales
 
         wo_q = []
+        wo_grouped = []
         up_grouped = {}
         up_q = {}
 
         def prepare_weights(it):
             if it == -LEAD:
-                wo_q.extend(quantise_weight(regroup_weight(nc.vector.tensor_copy, wo_raw), "wo"))
+                wo_grouped.append(new_grouped())
+                regroup_columns(nc.vector.tensor_copy, wo_grouped[0], wo_raw, 0, 352)
+                regroup_columns(nc.scalar.copy, wo_grouped[0], wo_raw, 352, 512)
+            if it == -LEAD + 1:
+                wo_q.extend(quantise_weight(wo_grouped[0], "wo"))
             c = it + LEAD - 1
             if 0 <= c < CHUNKS:
-                up_grouped[0, c] = regroup_weight(nc.vector.tensor_copy, up_raw[0][c])
-                up_grouped[1, c] = regroup_weight(nc.scalar.copy, up_raw[1][c])
+                for half, engine in ((0, nc.vector.tensor_copy), (1, nc.scalar.copy)):
+                    up_grouped[half, c] = new_grouped()
+                    regroup_columns(engine, up_grouped[half, c], up_raw[half][c], 0, N_PASS)
             if 0 <= c - 1 < CHUNKS:
                 for half in range(2):
                     up_q[half, c - 1] = quantise_weight(up_grouped[half, c - 1], "up%d_%d" % (half, c - 1))
@@ -127,109 +149,131 @@ def tile_model_pb_kernel(tc, o_attn, xm, attn_o_w, ffn_norm_w, ffn_up_w, out_0, 
         def in_range(j):
             return 0 <= j < TILES
 
-        def first_stage(it):
-            ja, jb, jc, je = it + 6, it + 5, it + 4, it + 2
-            if in_range(jb):
-                acc = psum.tile([P, D], F32, tag="acc")
+        def project(j):
+            codes, scales, cols = live["o", j]
+            acc = psum.tile([P, D], F32, tag="acc")
+            nc.tensor.matmul_mx(
+                out=acc[:],
+                lhsT=codes[:, cols].bitcast(FP8X4),
+                lhsT_scale=scales[:, cols],
+                rhs=wo_q[0][:].bitcast(FP8X4),
+                rhs_scale=wo_q[1][:],
+                start=True,
+                stop=True,
+            )
+            x2 = stage.tile([P, D], F32)
+            live["x2", j] = x2
+            nc.vector.tensor_tensor(out=x2[:], in0=acc[:], in1=xm_sb[j // PAIR][:, j % PAIR, :], op=ALU.add)
+            nc.sync.dma_start(out=x2_rows[:, j, :], in_=x2[:])
+
+        def mean_square(j):
+            squares = stage.tile([P, D], BF16)
+            mean_sq = stage.tile([P, 1], F32)
+            nc.scalar.activation(
+                out=squares[:], in_=live["x2", j][:], func=ACT.Square, scale=D**-0.5, accum_out=mean_sq[:]
+            )
+            shifted = stage.tile([P, 1], F32)
+            nc.gpsimd.tensor_scalar(
+                out=shifted[:], in0=mean_sq[:], scalar1=1.0, scalar2=EPS, op0=ALU.mult, op1=ALU.add
+            )
+            rstd = stage.tile([P, 1], F32)
+            live["rstd", j] = rstd
+            nc.gpsimd.tensor_tensor(out=rstd[:], in0=shifted[:], in1=neg_half[:], op=ALU.pow)
+
+        def normalise(j):
+            xn = stage.tile([P, 2, P, 2], BF16)
+            live["xn", j] = xn
+            by_half = live["x2", j][:].rearrange("p (m u e) -> p u m e", u=2, e=2)
+            for u in range(2):
+                nc.vector.scalar_tensor_tensor(
+                    out=xn[:, u, :, :],
+                    in0=by_half[:, u, :, :],
+                    scalar=live["rstd", j][:],
+                    in1=gain[:, u, :, :],
+                    op0=ALU.mult,
+                    op1=ALU.mult,
+                )
+
+        def transpose(it):
+            ja, je = it + 6, it + 2
+            kinds = []
+            turned = psum.tile([P, 2, 2, P], F32)
+            if in_range(ja):
+                words = o_sb[ja // PAIR][:].bitcast(F32)
+                for u in range(2):
+                    nc.tensor.transpose(turned[:, 0, u, :], words[:, ja % PAIR, u : D // 2 : 2], ident_f32[:])
+                kinds.append(0)
+            if in_range(je):
+                words = live["xn", je][:].rearrange("p u m e -> p (u m e)").bitcast(F32)
+                for u in range(2):
+                    nc.tensor.transpose(turned[:, 1, u, :], words[:, P * u : P * (u + 1)], ident_f32[:])
+                kinds.append(1)
+            if not kinds:
+                return
+            k0, k1 = kinds[0], kinds[-1] + 1
+            grouped = stage.tile([P, 2, D], BF16, align_bytes=64, name="turned_grouped")
+            live["grouped", it] = (grouped, k0, k1)
+            nc.scalar.copy(
+                out=grouped[:, k0:k1, :].bitcast(F32).rearrange("p k (r u) -> p k r u", u=2),
+                in_=turned[:, k0:k1, :, :].rearrange("p k u r -> p k r u"),
+            )
+
+        def quantise(it):
+            if ("grouped", it) not in live:
+                return
+            grouped, k0, k1 = live["grouped", it]
+            codes = stage.tile([P, 2 * P], U32, align_bytes=64, bufs=6)
+            scales = stage.tile([P, 2 * P], U8, align_bytes=64, bufs=6)
+            nc.vector.quantize_mx(
+                out=codes[:, P * k0 : P * k1].bitcast(FP8X4),
+                scales=scales[:, P * k0 : P * k1],
+                in_=grouped[:, k0:k1, :].rearrange("p k d -> p (k d)"),
+            )
+            live["o", it + 6] = (codes, scales, slice(0, P))
+            live["xn_q", it + 2] = (codes, scales, slice(P, 2 * P))
+
+        def gate(j, c, h):
+            codes, scales, cols = live["xn_q", j]
+            halves = []
+            for half in range(2):
+                u_ps = psum.tile([P, N_PASS], F32, name="u%d" % half, bufs=3)
                 nc.tensor.matmul_mx(
-                    out=acc[:],
-                    lhsT=live["o_codes", jb][:].bitcast(FP8X4),
-                    lhsT_scale=live["o_scales", jb][:],
-                    rhs=wo_q[0][:].bitcast(FP8X4),
-                    rhs_scale=wo_q[1][:],
+                    out=u_ps[:],
+                    lhsT=codes[:, cols].bitcast(FP8X4),
+                    lhsT_scale=scales[:, cols],
+                    rhs=up_q[half, c][0][:].bitcast(FP8X4),
+                    rhs_scale=up_q[half, c][1][:],
                     start=True,
                     stop=True,
                 )
-            if in_range(ja):
-                words = o_sb[ja // PAIR][:].bitcast(F32)
-                oT = psum.tile([P, 2, P], F32)
-                for u in range(2):
-                    nc.tensor.transpose(oT[:, u, :], words[:, ja % PAIR, u : D // 2 : 2], ident_f32[:])
-            if in_range(je):
-                xnT = psum.tile([P, PACK, P], BF16)
-                for t in range(PACK):
-                    nc.tensor.transpose(xnT[:, t, :], live["xn", je][:, t, :], ident_bf16[:])
-
-            if in_range(ja):
-                o_grouped = stage.tile([P, P * PACK], BF16, align_bytes=64)
-                nc.vector.tensor_copy(
-                    out=o_grouped[:].bitcast(F32).rearrange("p (r u) -> p r u", u=2),
-                    in_=oT[:].rearrange("p u r -> p r u"),
-                )
-            if in_range(jb):
-                x2 = stage.tile([P, D], F32)
-                live["x2", jb] = x2
-                nc.vector.tensor_tensor(out=x2[:], in0=acc[:], in1=xm_sb[jb // PAIR][:, jb % PAIR, :], op=ALU.add)
-                nc.sync.dma_start(out=x2_rows[:, jb, :], in_=x2[:])
-            if in_range(jc):
-                squares = stage.tile([P, D], BF16)
-                mean_sq = stage.tile([P, 1], F32)
-                nc.scalar.activation(
-                    out=squares[:], in_=live["x2", jc][:], func=ACT.Square, scale=D**-0.5, accum_out=mean_sq[:]
-                )
-                shifted = stage.tile([P, 1], F32)
-                nc.gpsimd.tensor_scalar(
-                    out=shifted[:], in0=mean_sq[:], scalar1=1.0, scalar2=EPS, op0=ALU.mult, op1=ALU.add
-                )
-                rstd = stage.tile([P, 1], F32)
-                nc.gpsimd.tensor_tensor(out=rstd[:], in0=shifted[:], in1=neg_half[:], op=ALU.pow)
-                xn = stage.tile([P, PACK, P], BF16)
-                live["xn", jc] = xn
-                nc.gpsimd.tensor_scalar(
-                    out=xn[:],
-                    in0=live["x2_gain", jc][:].rearrange("p (m t) -> p t m", t=PACK),
-                    scalar1=rstd[:], scalar2=1.0, op0=ALU.mult, op1=ALU.mult
-                )
-            if in_range(jb):
-                x2_gain = stage.tile([P, D], F32)
-                live["x2_gain", jb] = x2_gain
-                nc.gpsimd.tensor_tensor(out=x2_gain[:], in0=x2[:], in1=gain[:], op=ALU.mult)
-            if in_range(ja):
-                o_codes = stage.tile([P, P], U32, align_bytes=64)
-                o_scales = stage.tile([P, P], U8, align_bytes=64)
-                live["o_codes", ja] = o_codes
-                live["o_scales", ja] = o_scales
-                nc.vector.quantize_mx(out=o_codes[:].bitcast(FP8X4), scales=o_scales[:], in_=o_grouped[:])
-            if in_range(je):
-                xn_grouped = stage.tile([P, P, PACK], BF16, align_bytes=64)
-                nc.scalar.copy(out=xn_grouped[:], in_=xnT[:].rearrange("p t r -> p r t"))
-                xn_codes = stage.tile([P, P], U32, align_bytes=64)
-                xn_scales = stage.tile([P, P], U8, align_bytes=64)
-                live["xn_codes", je] = xn_codes
-                live["xn_scales", je] = xn_scales
-                nc.vector.quantize_mx(
-                    out=xn_codes[:].bitcast(FP8X4),
-                    scales=xn_scales[:],
-                    in_=xn_grouped[:].rearrange("p r t -> p (r t)"),
-                )
-
-        def second_stage(j):
-            h = results.tile([P, F], F32)
-            for c in range(CHUNKS):
-                halves = []
-                for half in range(2):
-                    codes, scales = up_q[half, c]
-                    u_ps = psum.tile([P, N_PASS], F32, name="u%d" % half, bufs=2 + half)
-                    nc.tensor.matmul_mx(
-                        out=u_ps[:],
-                        lhsT=live["xn_codes", j][:].bitcast(FP8X4),
-                        lhsT_scale=live["xn_scales", j][:],
-                        rhs=codes[:].bitcast(FP8X4),
-                        rhs_scale=scales[:],
-                        start=True,
-                        stop=True,
-                    )
-                    halves.append(u_ps)
-                silu = gated.tile([P, N_PASS], F32)
-                nc.scalar.activation(out=silu[:], in_=halves[0][:], func=ACT.Silu)
-                nc.vector.tensor_tensor(
-                    out=h[:, N_PASS * c : N_PASS * (c + 1)], in0=halves[1][:], in1=silu[:], op=ALU.mult
-                )
-            nc.sync.dma_start(out=h_rows[:, j, :], in_=h[:])
+                halves.append(u_ps)
+            silu = gated.tile([P, N_PASS], F32)
+            nc.scalar.activation(out=silu[:], in_=halves[0][:], func=ACT.Silu)
+            nc.vector.tensor_tensor(out=h[:, N_PASS * c : N_PASS * (c + 1)], in0=halves[1][:], in1=silu[:], op=ALU.mult)
 
         for it in range(-LEAD, TILES):
-            if it < 0:
-                prepare_weights(it)
-            else:
-                second_stage(it)
-            first_stage(it)
+            h = None
+            if it >= 0:
+                h = results.tile([P, F], F32)
+            for c in range(CHUNKS):
+                if it >= 0:
+                    gate(it, c, h)
+                if c == 0 and in_range(it + 4):
+                    project(it + 4)
+                if c == 1:
+                    transpose(it)
+                if c == 2 and in_range(it + 3):
+                    normalise(it + 3)
+                if c == 2 and it < 0:
+                    prepare_weights(it)
+                if c == 3 and in_range(it + 4):
+                    mean_square(it + 4)
+                if c == 3:
+                    quantise(it)
+            if it >= 0:
+                if it < TILES - 1:
+                    nc.sync.dma_start(out=h_rows[:, it, :], in_=h[:])
+                else:
+                    for c in range(CHUNKS):
+                        cols = slice(N_PASS * c, N_PASS * (c + 1))
+                        nc.sync.dma_start(out=h_rows[:, it, cols], in_=h[:, cols])

@@ -23,6 +23,7 @@ N_PASS = 512
 CHUNKS = F // N_PASS
 LEAD = 6
 EPS = 1e-5
+ON_GPSIMD = 3
 
 FLOPS = 2 * TOKENS * D * (D + 2 * F)
 
@@ -43,7 +44,7 @@ def tile_model_pb_kernel(tc, o_attn, xm, attn_o_w, ffn_norm_w, ffn_up_w, out_0, 
         regroup = ctx.enter_context(tc.tile_pool(name="regroup", bufs=4))
         stage = ctx.enter_context(tc.tile_pool(name="stage", bufs=4))
         gated = ctx.enter_context(tc.tile_pool(name="gated", bufs=4))
-        results = ctx.enter_context(tc.tile_pool(name="results", bufs=3))
+        results = ctx.enter_context(tc.tile_pool(name="results", bufs=6))
         psum = ctx.enter_context(tc.psum_pool(name="psum", bufs=1))
 
         gain_row = consts.tile([P, D], BF16)
@@ -85,8 +86,8 @@ def tile_model_pb_kernel(tc, o_attn, xm, attn_o_w, ffn_norm_w, ffn_up_w, out_0, 
         load_o(0)
         nc.sync.dma_start(out=gain_row[0:1, :], in_=ffn_norm_w.unsqueeze(0))
         nc.sync.dma_start(out=wo_raw[:], in_=wo_rows)
-        load_up(0)
         load_xm(0)
+        load_up(0)
         load_o(1)
         load_up(1)
         load_xm(1)
@@ -98,10 +99,6 @@ def tile_model_pb_kernel(tc, o_attn, xm, attn_o_w, ffn_norm_w, ffn_up_w, out_0, 
             load_o(i)
             load_xm(i)
 
-        gain_ps = psum.tile([P, D], F32, tag="acc")
-        nc.tensor.matmul(out=gain_ps[:], lhsT=ones[:], rhs=gain_row[:], start=True, stop=True)
-        gain = consts.tile([P, 2, P, 2], F32)
-        nc.vector.tensor_copy(out=gain[:], in_=gain_ps[:].rearrange("p (m u e) -> p u m e", u=2, e=2))
 
         def new_grouped():
             grouped = regroup.tile([P, N_PASS, PACK], BF16, tag="grouped", align_bytes=64)
@@ -128,21 +125,20 @@ def tile_model_pb_kernel(tc, o_attn, xm, attn_o_w, ffn_norm_w, ffn_up_w, out_0, 
         up_grouped = {}
         up_q = {}
 
-        def prepare_weights(it):
-            if it == -LEAD:
-                wo_grouped.append(new_grouped())
-                regroup_columns(nc.vector.tensor_copy, wo_grouped[0], wo_raw, 0, 352)
-                regroup_columns(nc.scalar.copy, wo_grouped[0], wo_raw, 352, 512)
-            if it == -LEAD + 1:
-                wo_q.extend(quantise_weight(wo_grouped[0], "wo"))
-            c = it + LEAD - 1
-            if 0 <= c < CHUNKS:
-                for half, engine in ((0, nc.vector.tensor_copy), (1, nc.scalar.copy)):
-                    up_grouped[half, c] = new_grouped()
-                    regroup_columns(engine, up_grouped[half, c], up_raw[half][c], 0, N_PASS)
-            if 0 <= c - 1 < CHUNKS:
-                for half in range(2):
-                    up_q[half, c - 1] = quantise_weight(up_grouped[half, c - 1], "up%d_%d" % (half, c - 1))
+        def prepare_wo():
+            wo_grouped.append(new_grouped())
+            regroup_columns(nc.vector.tensor_copy, wo_grouped[0], wo_raw, 0, 352)
+            regroup_columns(nc.scalar.copy, wo_grouped[0], wo_raw, 352, N_PASS)
+
+        def regroup_up(c, half):
+            up_grouped[half, c] = new_grouped()
+            if half:
+                regroup_columns(nc.scalar.copy, up_grouped[half, c], up_raw[half][c], 0, N_PASS)
+            else:
+                regroup_columns(nc.vector.tensor_copy, up_grouped[half, c], up_raw[half][c], 0, N_PASS)
+
+        def quantise_up(c, half):
+            up_q[half, c] = quantise_weight(up_grouped[half, c], "up%d_%d" % (half, c))
 
         live = {}
 
@@ -161,7 +157,11 @@ def tile_model_pb_kernel(tc, o_attn, xm, attn_o_w, ffn_norm_w, ffn_up_w, out_0, 
                 start=True,
                 stop=True,
             )
-            x2 = stage.tile([P, D], F32)
+            live["acc", j] = acc
+
+        def residual(j):
+            acc = live["acc", j]
+            x2 = stage.tile([P, D], F32, bufs=8)
             live["x2", j] = x2
             nc.vector.tensor_tensor(out=x2[:], in0=acc[:], in1=xm_sb[j // PAIR][:, j % PAIR, :], op=ALU.add)
             nc.sync.dma_start(out=x2_rows[:, j, :], in_=x2[:])
@@ -180,9 +180,29 @@ def tile_model_pb_kernel(tc, o_attn, xm, attn_o_w, ffn_norm_w, ffn_up_w, out_0, 
             live["rstd", j] = rstd
             nc.gpsimd.tensor_tensor(out=rstd[:], in0=shifted[:], in1=neg_half[:], op=ALU.pow)
 
+        def apply_gain(j):
+            x2_gain = stage.tile([P, 2, P, 2], F32)
+            live["x2_gain", j] = x2_gain
+            nc.gpsimd.tensor_tensor(
+                out=x2_gain[:],
+                in0=live["x2", j][:].rearrange("p (m u e) -> p u m e", u=2, e=2),
+                in1=gain[:],
+                op=ALU.mult,
+            )
+
         def normalise(j):
             xn = stage.tile([P, 2, P, 2], BF16)
             live["xn", j] = xn
+            if j >= ON_GPSIMD:
+                nc.gpsimd.tensor_scalar(
+                    out=xn[:],
+                    in0=live["x2_gain", j][:],
+                    scalar1=live["rstd", j][:],
+                    scalar2=1.0,
+                    op0=ALU.mult,
+                    op1=ALU.mult,
+                )
+                return
             by_half = live["x2", j][:].rearrange("p (m u e) -> p u m e", u=2, e=2)
             for u in range(2):
                 nc.vector.scalar_tensor_tensor(
@@ -208,15 +228,21 @@ def tile_model_pb_kernel(tc, o_attn, xm, attn_o_w, ffn_norm_w, ffn_up_w, out_0, 
                 for u in range(2):
                     nc.tensor.transpose(turned[:, 1, u, :], words[:, P * u : P * (u + 1)], ident_f32[:])
                 kinds.append(1)
+            live["turned", it] = (turned, kinds)
+
+        def collect(it):
+            turned, kinds = live["turned", it]
             if not kinds:
                 return
             k0, k1 = kinds[0], kinds[-1] + 1
             grouped = stage.tile([P, 2, D], BF16, align_bytes=64, name="turned_grouped")
             live["grouped", it] = (grouped, k0, k1)
-            nc.scalar.copy(
-                out=grouped[:, k0:k1, :].bitcast(F32).rearrange("p k (r u) -> p k r u", u=2),
-                in_=turned[:, k0:k1, :, :].rearrange("p k u r -> p k r u"),
-            )
+            for k in kinds:
+                copy_engine = nc.scalar.copy if k or it < 0 or it % 2 else nc.vector.tensor_copy
+                copy_engine(
+                    out=grouped[:, k, :].bitcast(F32).rearrange("p (r u) -> p r u", u=2),
+                    in_=turned[:, k, :, :].rearrange("p u r -> p r u"),
+                )
 
         def quantise(it):
             if ("grouped", it) not in live:
@@ -251,29 +277,92 @@ def tile_model_pb_kernel(tc, o_attn, xm, attn_o_w, ffn_norm_w, ffn_up_w, out_0, 
             nc.scalar.activation(out=silu[:], in_=halves[0][:], func=ACT.Silu)
             nc.vector.tensor_tensor(out=h[:, N_PASS * c : N_PASS * (c + 1)], in0=halves[1][:], in1=silu[:], op=ALU.mult)
 
+        gain = consts.tile([P, 2, P, 2], F32)
+
+        def spread_gain():
+            gain_ps = psum.tile([P, D], F32, tag="acc")
+            nc.tensor.matmul(out=gain_ps[:], lhsT=ones[:], rhs=gain_row[:], start=True, stop=True)
+            nc.vector.tensor_copy(out=gain[:], in_=gain_ps[:].rearrange("p (m u e) -> p u m e", u=2, e=2))
+
+        h_tiles = {}
+
+        def units(it):
+            if it < 0:
+                return []
+            if it < CHUNKS:
+                return [(it, c) for c in range(it)] + [(j, it) for j in range(it + 1)]
+            return [(it, c) for c in range(CHUNKS)]
+
+        def run_unit(j, c):
+            if c == 0:
+                h_tiles[j] = results.tile([P, F], F32, name="h")
+            gate(j, c, h_tiles[j])
+            first = c - c % 2 if j < TILES - 1 else c
+            if c % 2 == 1 or j == TILES - 1:
+                cols = slice(N_PASS * first, N_PASS * (c + 1))
+                nc.sync.dma_start(out=h_rows[:, j, cols], in_=h_tiles[j][:, cols])
+
         for it in range(-LEAD, TILES):
-            h = None
-            if it >= 0:
-                h = results.tile([P, F], F32)
-            for c in range(CHUNKS):
-                if it >= 0:
-                    gate(it, c, h)
-                if c == 0 and in_range(it + 4):
-                    project(it + 4)
+            todo = units(it)
+            for c in range(CHUNKS + 1):
+                if c == 0:
+                    if in_range(it + 4):
+                        project(it + 4)
+                    if in_range(it + 4):
+                        residual(it + 4)
+                    if in_range(it + 4):
+                        if it + 4 >= ON_GPSIMD:
+                            apply_gain(it + 4)
+                    if in_range(it + 3):
+                        normalise(it + 3)
+                    for j, chunk in todo[len(todo) * 0 // CHUNKS : len(todo) * 1 // CHUNKS]:
+                        run_unit(j, chunk)
                 if c == 1:
+                    if it == -5:
+                        wo_q.extend(quantise_weight(wo_grouped[0], "wo"))
+                    if it == 0:
+                        regroup_up(3, 0)
+                    if it == 1:
+                        quantise_up(3, 0)
+                    for j, chunk in todo[len(todo) * 1 // CHUNKS : len(todo) * 2 // CHUNKS]:
+                        run_unit(j, chunk)
+                if c == 2:
                     transpose(it)
-                if c == 2 and in_range(it + 3):
-                    normalise(it + 3)
-                if c == 2 and it < 0:
-                    prepare_weights(it)
-                if c == 3 and in_range(it + 4):
-                    mean_square(it + 4)
+                    collect(it)
+                    if it == -5:
+                        regroup_up(0, 0)
+                    if it == -3:
+                        quantise_up(0, 1)
+                    if it == -2:
+                        quantise_up(1, 0)
+                    for j, chunk in todo[len(todo) * 2 // CHUNKS : len(todo) * 3 // CHUNKS]:
+                        run_unit(j, chunk)
                 if c == 3:
                     quantise(it)
-            if it >= 0:
-                if it < TILES - 1:
-                    nc.sync.dma_start(out=h_rows[:, it, :], in_=h[:])
-                else:
-                    for c in range(CHUNKS):
-                        cols = slice(N_PASS * c, N_PASS * (c + 1))
-                        nc.sync.dma_start(out=h_rows[:, it, cols], in_=h[:, cols])
+                    if it == -6:
+                        prepare_wo()
+                        spread_gain()
+                    if it == -4:
+                        quantise_up(0, 0)
+                        regroup_up(1, 0)
+                    if it == -3:
+                        regroup_up(1, 1)
+                    if it == -2:
+                        regroup_up(2, 0)
+                        quantise_up(1, 1)
+                    if it == -1:
+                        regroup_up(2, 1)
+                    if it == 0:
+                        regroup_up(3, 1)
+                        quantise_up(2, 1)
+                    if it == 1:
+                        quantise_up(3, 1)
+                    for j, chunk in todo[len(todo) * 3 // CHUNKS : len(todo) * 4 // CHUNKS]:
+                        run_unit(j, chunk)
+                if c == 4:
+                    if in_range(it + 4):
+                        mean_square(it + 4)
+                    if it == -5:
+                        regroup_up(0, 1)
+                    if it == -1:
+                        quantise_up(2, 0)

@@ -23,7 +23,6 @@ N_PASS = 512
 CHUNKS = F // N_PASS
 LEAD = 6
 EPS = 1e-5
-ON_GPSIMD = 3
 
 FLOPS = 2 * TOKENS * D * (D + 2 * F)
 
@@ -180,29 +179,9 @@ def tile_model_pb_kernel(tc, o_attn, xm, attn_o_w, ffn_norm_w, ffn_up_w, out_0, 
             live["rstd", j] = rstd
             nc.gpsimd.tensor_tensor(out=rstd[:], in0=shifted[:], in1=neg_half[:], op=ALU.pow)
 
-        def apply_gain(j):
-            x2_gain = stage.tile([P, 2, P, 2], F32)
-            live["x2_gain", j] = x2_gain
-            nc.gpsimd.tensor_tensor(
-                out=x2_gain[:],
-                in0=live["x2", j][:].rearrange("p (m u e) -> p u m e", u=2, e=2),
-                in1=gain[:],
-                op=ALU.mult,
-            )
-
         def normalise(j):
             xn = stage.tile([P, 2, P, 2], BF16)
             live["xn", j] = xn
-            if j >= ON_GPSIMD:
-                nc.gpsimd.tensor_scalar(
-                    out=xn[:],
-                    in0=live["x2_gain", j][:],
-                    scalar1=live["rstd", j][:],
-                    scalar2=1.0,
-                    op0=ALU.mult,
-                    op1=ALU.mult,
-                )
-                return
             by_half = live["x2", j][:].rearrange("p (m u e) -> p u m e", u=2, e=2)
             for u in range(2):
                 nc.vector.scalar_tensor_tensor(
@@ -237,12 +216,10 @@ def tile_model_pb_kernel(tc, o_attn, xm, attn_o_w, ffn_norm_w, ffn_up_w, out_0, 
             k0, k1 = kinds[0], kinds[-1] + 1
             grouped = stage.tile([P, 2, D], BF16, align_bytes=64, name="turned_grouped")
             live["grouped", it] = (grouped, k0, k1)
-            for k in kinds:
-                copy_engine = nc.scalar.copy if k or it < 0 or it % 2 else nc.vector.tensor_copy
-                copy_engine(
-                    out=grouped[:, k, :].bitcast(F32).rearrange("p (r u) -> p r u", u=2),
-                    in_=turned[:, k, :, :].rearrange("p u r -> p r u"),
-                )
+            nc.scalar.copy(
+                out=grouped[:, k0:k1, :].bitcast(F32).rearrange("p k (r u) -> p k r u", u=2),
+                in_=turned[:, k0:k1, :, :].rearrange("p k u r -> p k r u"),
+            )
 
         def quantise(it):
             if ("grouped", it) not in live:
@@ -310,14 +287,11 @@ def tile_model_pb_kernel(tc, o_attn, xm, attn_o_w, ffn_norm_w, ffn_up_w, out_0, 
                         project(it + 4)
                     if in_range(it + 4):
                         residual(it + 4)
-                    if in_range(it + 4):
-                        if it + 4 >= ON_GPSIMD:
-                            apply_gain(it + 4)
-                    if in_range(it + 3):
-                        normalise(it + 3)
                     for j, chunk in todo[len(todo) * 0 // CHUNKS : len(todo) * 1 // CHUNKS]:
                         run_unit(j, chunk)
                 if c == 1:
+                    if in_range(it + 3):
+                        mean_square(it + 3)
                     if it == -5:
                         wo_q.extend(quantise_weight(wo_grouped[0], "wo"))
                     if it == 0:
@@ -328,7 +302,6 @@ def tile_model_pb_kernel(tc, o_attn, xm, attn_o_w, ffn_norm_w, ffn_up_w, out_0, 
                         run_unit(j, chunk)
                 if c == 2:
                     transpose(it)
-                    collect(it)
                     if it == -5:
                         regroup_up(0, 0)
                     if it == -3:
@@ -338,7 +311,9 @@ def tile_model_pb_kernel(tc, o_attn, xm, attn_o_w, ffn_norm_w, ffn_up_w, out_0, 
                     for j, chunk in todo[len(todo) * 2 // CHUNKS : len(todo) * 3 // CHUNKS]:
                         run_unit(j, chunk)
                 if c == 3:
-                    quantise(it)
+                    collect(it)
+                    if in_range(it + 3):
+                        normalise(it + 3)
                     if it == -6:
                         prepare_wo()
                         spread_gain()
@@ -360,8 +335,7 @@ def tile_model_pb_kernel(tc, o_attn, xm, attn_o_w, ffn_norm_w, ffn_up_w, out_0, 
                     for j, chunk in todo[len(todo) * 3 // CHUNKS : len(todo) * 4 // CHUNKS]:
                         run_unit(j, chunk)
                 if c == 4:
-                    if in_range(it + 4):
-                        mean_square(it + 4)
+                    quantise(it)
                     if it == -5:
                         regroup_up(0, 1)
                     if it == -1:

@@ -23,6 +23,7 @@ N_PASS = 512
 CHUNKS = F // N_PASS
 LEAD = 6
 EPS = 1e-5
+X2_RING = 8
 
 FLOPS = 2 * TOKENS * D * (D + 2 * F)
 
@@ -141,6 +142,9 @@ def tile_model_pb_kernel(tc, o_attn, xm, attn_o_w, ffn_norm_w, ffn_up_w, out_0, 
 
         live = {}
 
+        x2_ring = consts.tile([P, X2_RING, D + 8], F32)
+        nc.vector.memset(x2_ring[:, :, D : D + 1], (D * EPS) ** 0.5)
+
         def in_range(j):
             return 0 <= j < TILES
 
@@ -160,38 +164,27 @@ def tile_model_pb_kernel(tc, o_attn, xm, attn_o_w, ffn_norm_w, ffn_up_w, out_0, 
 
         def residual(j):
             acc = live["acc", j]
-            x2 = stage.tile([P, D], F32, bufs=8)
+            x2 = x2_ring[:, j % X2_RING, :D]
             live["x2", j] = x2
-            nc.vector.tensor_tensor(out=x2[:], in0=acc[:], in1=xm_sb[j // PAIR][:, j % PAIR, :], op=ALU.add)
-            nc.sync.dma_start(out=x2_rows[:, j, :], in_=x2[:])
+            nc.vector.tensor_tensor(out=x2, in0=acc[:], in1=xm_sb[j // PAIR][:, j % PAIR, :], op=ALU.add)
+            nc.sync.dma_start(out=x2_rows[:, j, :], in_=x2)
 
         def mean_square(j):
-            squares = stage.tile([P, D], BF16)
+            squares = stage.tile([P, D + 1], BF16)
             mean_sq = stage.tile([P, 1], F32)
             nc.scalar.activation(
-                out=squares[:], in_=live["x2", j][:], func=ACT.Square, scale=D**-0.5, accum_out=mean_sq[:]
-            )
-            shifted = stage.tile([P, 1], F32)
-            nc.gpsimd.tensor_scalar(
-                out=shifted[:], in0=mean_sq[:], scalar1=1.0, scalar2=EPS, op0=ALU.mult, op1=ALU.add
+                out=squares[:], in_=x2_ring[:, j % X2_RING, : D + 1], func=ACT.Square, scale=D**-0.5, accum_out=mean_sq[:]
             )
             rstd = stage.tile([P, 1], F32)
             live["rstd", j] = rstd
-            nc.gpsimd.tensor_tensor(out=rstd[:], in0=shifted[:], in1=neg_half[:], op=ALU.pow)
+            nc.gpsimd.tensor_tensor(out=rstd[:], in0=mean_sq[:], in1=neg_half[:], op=ALU.pow)
 
         def normalise(j):
-            xn = stage.tile([P, 2, P, 2], BF16)
+            xn = stage.tile([P, D], BF16)
             live["xn", j] = xn
-            by_half = live["x2", j][:].rearrange("p (m u e) -> p u m e", u=2, e=2)
-            for u in range(2):
-                nc.vector.scalar_tensor_tensor(
-                    out=xn[:, u, :, :],
-                    in0=by_half[:, u, :, :],
-                    scalar=live["rstd", j][:],
-                    in1=gain[:, u, :, :],
-                    op0=ALU.mult,
-                    op1=ALU.mult,
-                )
+            nc.vector.scalar_tensor_tensor(
+                out=xn[:], in0=live["x2", j], scalar=live["rstd", j][:], in1=gain[:], op0=ALU.mult, op1=ALU.mult
+            )
 
         def transpose(it):
             ja, je = it + 6, it + 2
@@ -203,9 +196,9 @@ def tile_model_pb_kernel(tc, o_attn, xm, attn_o_w, ffn_norm_w, ffn_up_w, out_0, 
                     nc.tensor.transpose(turned[:, 0, u, :], words[:, ja % PAIR, u : D // 2 : 2], ident_f32[:])
                 kinds.append(0)
             if in_range(je):
-                words = live["xn", je][:].rearrange("p u m e -> p (u m e)").bitcast(F32)
+                words = live["xn", je][:].bitcast(F32)
                 for u in range(2):
-                    nc.tensor.transpose(turned[:, 1, u, :], words[:, P * u : P * (u + 1)], ident_f32[:])
+                    nc.tensor.transpose(turned[:, 1, u, :], words[:, u : D // 2 : 2], ident_f32[:])
                 kinds.append(1)
             live["turned", it] = (turned, kinds)
 
@@ -235,31 +228,34 @@ def tile_model_pb_kernel(tc, o_attn, xm, attn_o_w, ffn_norm_w, ffn_up_w, out_0, 
             live["o", it + 6] = (codes, scales, slice(0, P))
             live["xn_q", it + 2] = (codes, scales, slice(P, 2 * P))
 
-        def gate(j, c, h):
+        def gate(j, h, first, width):
             codes, scales, cols = live["xn_q", j]
+            c, offset = divmod(first, N_PASS)
             halves = []
             for half in range(2):
                 u_ps = psum.tile([P, N_PASS], F32, name="u%d" % half, bufs=3)
                 nc.tensor.matmul_mx(
-                    out=u_ps[:],
+                    out=u_ps[:, :width],
                     lhsT=codes[:, cols].bitcast(FP8X4),
                     lhsT_scale=scales[:, cols],
-                    rhs=up_q[half, c][0][:].bitcast(FP8X4),
-                    rhs_scale=up_q[half, c][1][:],
+                    rhs=up_q[half, c][0][:, offset : offset + width].bitcast(FP8X4),
+                    rhs_scale=up_q[half, c][1][:, offset : offset + width],
                     start=True,
                     stop=True,
                 )
                 halves.append(u_ps)
             silu = gated.tile([P, N_PASS], F32)
-            nc.scalar.activation(out=silu[:], in_=halves[0][:], func=ACT.Silu)
-            nc.vector.tensor_tensor(out=h[:, N_PASS * c : N_PASS * (c + 1)], in0=halves[1][:], in1=silu[:], op=ALU.mult)
+            nc.scalar.activation(out=silu[:, :width], in_=halves[0][:, :width], func=ACT.Silu)
+            nc.vector.tensor_tensor(
+                out=h[:, first : first + width], in0=halves[1][:, :width], in1=silu[:, :width], op=ALU.mult
+            )
 
-        gain = consts.tile([P, 2, P, 2], F32)
+        gain = consts.tile([P, D], F32)
 
         def spread_gain():
             gain_ps = psum.tile([P, D], F32, tag="acc")
             nc.tensor.matmul(out=gain_ps[:], lhsT=ones[:], rhs=gain_row[:], start=True, stop=True)
-            nc.vector.tensor_copy(out=gain[:], in_=gain_ps[:].rearrange("p (m u e) -> p u m e", u=2, e=2))
+            nc.vector.tensor_copy(out=gain[:], in_=gain_ps[:])
 
         h_tiles = {}
 
@@ -273,11 +269,17 @@ def tile_model_pb_kernel(tc, o_attn, xm, attn_o_w, ffn_norm_w, ffn_up_w, out_0, 
         def run_unit(j, c):
             if c == 0:
                 h_tiles[j] = results.tile([P, F], F32, name="h")
-            gate(j, c, h_tiles[j])
-            first = c - c % 2 if j < TILES - 1 else c
-            if c % 2 == 1 or j == TILES - 1:
-                cols = slice(N_PASS * first, N_PASS * (c + 1))
-                nc.sync.dma_start(out=h_rows[:, j, cols], in_=h_tiles[j][:, cols])
+            h = h_tiles[j]
+            pieces = 2 if (j, c) == (TILES - 1, CHUNKS - 1) else 1
+            for i in range(pieces):
+                width = N_PASS // pieces
+                gate(j, h, N_PASS * c + width * i, width)
+                if j == TILES - 1:
+                    cols = slice(N_PASS * c + width * i, N_PASS * c + width * (i + 1))
+                    nc.sync.dma_start(out=h_rows[:, j, cols], in_=h[:, cols])
+            if j < TILES - 1 and c % 2 == 1:
+                cols = slice(N_PASS * (c - 1), N_PASS * (c + 1))
+                nc.sync.dma_start(out=h_rows[:, j, cols], in_=h[:, cols])
 
         for it in range(-LEAD, TILES):
             todo = units(it)

@@ -17,13 +17,13 @@ D = P * PACK
 TOKENS = 4 * 576
 TILES = TOKENS // P
 PAIR = 2
-PAIRS = TILES // PAIR
 F = 2048
 N_PASS = 512
 CHUNKS = F // N_PASS
 LEAD = 6
 EPS = 1e-5
-X2_RING = 8
+X2_RING = 5
+X2_PAD = 8
 
 FLOPS = 2 * TOKENS * D * (D + 2 * F)
 
@@ -60,44 +60,51 @@ def tile_model_pb_kernel(tc, o_attn, xm, attn_o_w, ffn_norm_w, ffn_up_w, out_0, 
         neg_half = consts.tile([P, 1], F32)
         nc.vector.memset(neg_half[:], -0.5)
 
-        o_sb = []
-        xm_sb = []
+        groups = ((0, 2), (2, 4), (4, 6), (6, 12), (12, 18))
+        o_sb = {}
+        xm_sb = {}
 
-        def load_o(i):
-            o_sb.append(loads.tile([P, PAIR, D], BF16, name="o_sb%d" % i))
-            nc.sync.dma_start(out=o_sb[i][:], in_=o_rows[:, PAIR * i : PAIR * (i + 1), :])
+        def load_tokens(name, rows, where, g):
+            first, last = groups[g]
+            group = loads.tile([P, last - first, D], BF16, name="%s%d" % (name, g))
+            nc.sync.dma_start(out=group[:], in_=rows[:, first:last, :])
+            for j in range(first, last):
+                where[j] = group[:, j - first, :]
 
-        def load_xm(i):
-            xm_sb.append(loads.tile([P, PAIR, D], BF16, name="xm_sb%d" % i))
-            nc.sync.dma_start(out=xm_sb[i][:], in_=xm_rows[:, PAIR * i : PAIR * (i + 1), :])
+        def load_o(g):
+            load_tokens("o_sb", o_rows, o_sb, g)
+
+        def load_xm(g):
+            load_tokens("xm_sb", xm_rows, xm_sb, g)
 
         wo_rows = attn_o_w.rearrange("(p t) n -> p t n", t=PACK)
         up_rows = ffn_up_w.rearrange("(p t) n -> p t n", t=PACK)
         wo_raw = loads.tile([P, PACK, D], BF16)
         up_raw = [[], []]
 
-        def load_up(c):
+        def load_up(first_chunk, chunks):
             for half in range(2):
-                raw = loads.tile([P, PACK, N_PASS], BF16, name="up_raw%d_%d" % (half, c))
-                first = F * half + N_PASS * c
-                nc.sync.dma_start(out=raw[:], in_=up_rows[:, :, first : first + N_PASS])
-                up_raw[half].append(raw)
+                raw = loads.tile([P, PACK, chunks * N_PASS], BF16, name="up_raw%d_%d" % (half, first_chunk))
+                first = F * half + N_PASS * first_chunk
+                nc.sync.dma_start(out=raw[:], in_=up_rows[:, :, first : first + chunks * N_PASS])
+                for i in range(chunks):
+                    up_raw[half].append(raw[:, :, N_PASS * i : N_PASS * (i + 1)])
 
         load_o(0)
         nc.sync.dma_start(out=gain_row[0:1, :], in_=ffn_norm_w.unsqueeze(0))
         nc.sync.dma_start(out=wo_raw[:], in_=wo_rows)
         load_xm(0)
-        load_up(0)
+        load_up(0, 1)
         load_o(1)
-        load_up(1)
+        load_up(1, 1)
         load_xm(1)
         load_o(2)
-        load_up(2)
+        load_up(2, 2)
         load_xm(2)
-        load_up(3)
-        for i in range(3, PAIRS):
-            load_o(i)
-            load_xm(i)
+        load_o(3)
+        load_xm(3)
+        load_o(4)
+        load_xm(4)
 
 
         def new_grouped():
@@ -142,8 +149,9 @@ def tile_model_pb_kernel(tc, o_attn, xm, attn_o_w, ffn_norm_w, ffn_up_w, out_0, 
 
         live = {}
 
-        x2_ring = consts.tile([P, X2_RING, D + 8], F32)
-        nc.vector.memset(x2_ring[:, :, D : D + 1], (D * EPS) ** 0.5)
+        x2_ring = consts.tile([P, X2_RING, PAIR * D + 2 * X2_PAD], F32)
+        for column in (X2_PAD - 1, X2_PAD + PAIR * D):
+            nc.vector.memset(x2_ring[:, :, column : column + 1], (D * EPS) ** 0.5)
 
         def in_range(j):
             return 0 <= j < TILES
@@ -164,16 +172,22 @@ def tile_model_pb_kernel(tc, o_attn, xm, attn_o_w, ffn_norm_w, ffn_up_w, out_0, 
 
         def residual(j):
             acc = live["acc", j]
-            x2 = x2_ring[:, j % X2_RING, :D]
+            start = X2_PAD + D * (j % PAIR)
+            x2 = x2_ring[:, j // PAIR % X2_RING, start : start + D]
             live["x2", j] = x2
-            nc.vector.tensor_tensor(out=x2, in0=acc[:], in1=xm_sb[j // PAIR][:, j % PAIR, :], op=ALU.add)
-            nc.sync.dma_start(out=x2_rows[:, j, :], in_=x2)
+            nc.vector.tensor_tensor(out=x2, in0=acc[:], in1=xm_sb[j], op=ALU.add)
+            if j % PAIR == PAIR - 1:
+                nc.sync.dma_start(
+                    out=x2_rows[:, j - 1 : j + 1, :].rearrange("p j d -> p (j d)"),
+                    in_=x2_ring[:, j // PAIR % X2_RING, X2_PAD : X2_PAD + PAIR * D],
+                )
 
         def mean_square(j):
             squares = stage.tile([P, D + 1], BF16)
             mean_sq = stage.tile([P, 1], F32)
+            start = X2_PAD - 1 if j % PAIR == 0 else X2_PAD + D
             nc.scalar.activation(
-                out=squares[:], in_=x2_ring[:, j % X2_RING, : D + 1], func=ACT.Square, scale=D**-0.5, accum_out=mean_sq[:]
+                out=squares[:], in_=x2_ring[:, j // PAIR % X2_RING, start : start + D + 1], func=ACT.Square, scale=D**-0.5, accum_out=mean_sq[:]
             )
             rstd = stage.tile([P, 1], F32)
             live["rstd", j] = rstd
@@ -191,9 +205,9 @@ def tile_model_pb_kernel(tc, o_attn, xm, attn_o_w, ffn_norm_w, ffn_up_w, out_0, 
             kinds = []
             turned = psum.tile([P, 2, 2, P], F32)
             if in_range(ja):
-                words = o_sb[ja // PAIR][:].bitcast(F32)
+                words = o_sb[ja].bitcast(F32)
                 for u in range(2):
-                    nc.tensor.transpose(turned[:, 0, u, :], words[:, ja % PAIR, u : D // 2 : 2], ident_f32[:])
+                    nc.tensor.transpose(turned[:, 0, u, :], words[:, u : D // 2 : 2], ident_f32[:])
                 kinds.append(0)
             if in_range(je):
                 words = live["xn", je][:].bitcast(F32)
@@ -277,7 +291,10 @@ def tile_model_pb_kernel(tc, o_attn, xm, attn_o_w, ffn_norm_w, ffn_up_w, out_0, 
                 if j == TILES - 1:
                     cols = slice(N_PASS * c + width * i, N_PASS * c + width * (i + 1))
                     nc.sync.dma_start(out=h_rows[:, j, cols], in_=h[:, cols])
-            if j < TILES - 1 and c % 2 == 1:
+            whole = CHUNKS <= j < TILES - 5
+            if whole and c == CHUNKS - 1:
+                nc.sync.dma_start(out=h_rows[:, j, :], in_=h[:])
+            elif not whole and j < TILES - 1 and c % 2 == 1:
                 cols = slice(N_PASS * (c - 1), N_PASS * (c + 1))
                 nc.sync.dma_start(out=h_rows[:, j, cols], in_=h[:, cols])
 

@@ -43,7 +43,7 @@ def tile_model_pb_kernel(tc, o_attn, xm, attn_o_w, ffn_norm_w, ffn_up_w, out_0, 
         weights = ctx.enter_context(tc.tile_pool(name="weights", bufs=1))
         regroup = ctx.enter_context(tc.tile_pool(name="regroup", bufs=4))
         stage = ctx.enter_context(tc.tile_pool(name="stage", bufs=4))
-        gated = ctx.enter_context(tc.tile_pool(name="gated", bufs=4))
+        gated = ctx.enter_context(tc.tile_pool(name="gated", bufs=6))
         results = ctx.enter_context(tc.tile_pool(name="results", bufs=6))
         psum = ctx.enter_context(tc.psum_pool(name="psum", bufs=1))
 
@@ -242,27 +242,44 @@ def tile_model_pb_kernel(tc, o_attn, xm, attn_o_w, ffn_norm_w, ffn_up_w, out_0, 
             live["o", it + 6] = (codes, scales, slice(0, P))
             live["xn_q", it + 2] = (codes, scales, slice(P, 2 * P))
 
-        def gate(j, h, first, width):
+        def pass_of(half, j, first, width):
             codes, scales, cols = live["xn_q", j]
             c, offset = divmod(first, N_PASS)
-            halves = []
-            for half in range(2):
-                u_ps = psum.tile([P, N_PASS], F32, name="u%d" % half, bufs=3)
-                nc.tensor.matmul_mx(
-                    out=u_ps[:, :width],
-                    lhsT=codes[:, cols].bitcast(FP8X4),
-                    lhsT_scale=scales[:, cols],
-                    rhs=up_q[half, c][0][:, offset : offset + width].bitcast(FP8X4),
-                    rhs_scale=up_q[half, c][1][:, offset : offset + width],
-                    start=True,
-                    stop=True,
-                )
-                halves.append(u_ps)
-            silu = gated.tile([P, N_PASS], F32)
-            nc.scalar.activation(out=silu[:, :width], in_=halves[0][:, :width], func=ACT.Silu)
-            nc.vector.tensor_tensor(
-                out=h[:, first : first + width], in0=halves[1][:, :width], in1=silu[:, :width], op=ALU.mult
+            u_ps = psum.tile([P, N_PASS], F32, name="u%d" % half, bufs=3)
+            nc.tensor.matmul_mx(
+                out=u_ps[:, :width],
+                lhsT=codes[:, cols].bitcast(FP8X4),
+                lhsT_scale=scales[:, cols],
+                rhs=up_q[half, c][0][:, offset : offset + width].bitcast(FP8X4),
+                rhs_scale=up_q[half, c][1][:, offset : offset + width],
+                start=True,
+                stop=True,
             )
+            return u_ps
+
+        def start_unit(j, first, width):
+            silu = gated.tile([P, N_PASS], F32)
+            live["silu", j, first] = silu
+            u_ps = pass_of(0, j, first, width)
+            nc.scalar.activation(out=silu[:, :width], in_=u_ps[:, :width], func=ACT.Silu)
+
+        def finish_unit(j, first, width):
+            if first == 0:
+                h_tiles[j] = results.tile([P, F], F32, name="h")
+            h = h_tiles[j]
+            u_ps = pass_of(1, j, first, width)
+            nc.vector.tensor_tensor(
+                out=h[:, first : first + width], in0=u_ps[:, :width], in1=live["silu", j, first][:, :width], op=ALU.mult
+            )
+            last = first + width
+            if j == TILES - 1:
+                store_from = first
+            elif CHUNKS <= j < TILES - 5:
+                store_from = 0 if last == F else last
+            else:
+                store_from = last - F // 2 if last % (F // 2) == 0 else last
+            if store_from < last:
+                nc.sync.dma_start(out=h_rows[:, j, store_from:last], in_=h[:, store_from:last])
 
         gain = consts.tile([P, D], F32)
 
@@ -280,23 +297,25 @@ def tile_model_pb_kernel(tc, o_attn, xm, attn_o_w, ffn_norm_w, ffn_up_w, out_0, 
                 return [(it, c) for c in range(it)] + [(j, it) for j in range(it + 1)]
             return [(it, c) for c in range(CHUNKS)]
 
-        def run_unit(j, c):
-            if c == 0:
-                h_tiles[j] = results.tile([P, F], F32, name="h")
-            h = h_tiles[j]
-            pieces = 2 if (j, c) == (TILES - 1, CHUNKS - 1) else 1
-            for i in range(pieces):
+        order = []
+        for it in range(TILES):
+            for j, c in units(it):
+                pieces = 2 if (j, c) == (TILES - 1, CHUNKS - 1) else 1
                 width = N_PASS // pieces
-                gate(j, h, N_PASS * c + width * i, width)
-                if j == TILES - 1:
-                    cols = slice(N_PASS * c + width * i, N_PASS * c + width * (i + 1))
-                    nc.sync.dma_start(out=h_rows[:, j, cols], in_=h[:, cols])
-            whole = CHUNKS <= j < TILES - 5
-            if whole and c == CHUNKS - 1:
-                nc.sync.dma_start(out=h_rows[:, j, :], in_=h[:])
-            elif not whole and j < TILES - 1 and c % 2 == 1:
-                cols = slice(N_PASS * (c - 1), N_PASS * (c + 1))
-                nc.sync.dma_start(out=h_rows[:, j, cols], in_=h[:, cols])
+                order.extend((j, N_PASS * c + width * i, width) for i in range(pieces))
+        started = []
+        finished = []
+
+        def run_units(count):
+            for k in range(count):
+                ahead = len(finished) + 1
+                while len(started) < min(ahead + 1, len(order)):
+                    unit = order[len(started)]
+                    start_unit(unit[0], unit[1], unit[2])
+                    started.append(unit)
+                unit = order[len(finished)]
+                finish_unit(unit[0], unit[1], unit[2])
+                finished.append(unit)
 
         for it in range(-LEAD, TILES):
             todo = units(it)
@@ -306,56 +325,54 @@ def tile_model_pb_kernel(tc, o_attn, xm, attn_o_w, ffn_norm_w, ffn_up_w, out_0, 
                         project(it + 4)
                     if in_range(it + 4):
                         residual(it + 4)
-                    for j, chunk in todo[len(todo) * 0 // CHUNKS : len(todo) * 1 // CHUNKS]:
-                        run_unit(j, chunk)
+                    if it == -5:
+                        regroup_up(0, 0)
+                    if it == -4:
+                        regroup_up(0, 1)
+                    if it == 1:
+                        quantise_up(3, 0)
+                        regroup_up(3, 1)
+                    run_units(len(todo) * 1 // CHUNKS - len(todo) * 0 // CHUNKS)
                 if c == 1:
                     if in_range(it + 3):
                         mean_square(it + 3)
-                    if it == -5:
-                        wo_q.extend(quantise_weight(wo_grouped[0], "wo"))
+                    if it == -4:
+                        quantise_up(0, 0)
+                    if it == -3:
+                        regroup_up(1, 1)
+                    if it == -1:
+                        regroup_up(2, 1)
                     if it == 0:
                         regroup_up(3, 0)
-                    if it == 1:
-                        quantise_up(3, 0)
-                    for j, chunk in todo[len(todo) * 1 // CHUNKS : len(todo) * 2 // CHUNKS]:
-                        run_unit(j, chunk)
+                    run_units(len(todo) * 2 // CHUNKS - len(todo) * 1 // CHUNKS)
                 if c == 2:
-                    transpose(it)
-                    if it == -5:
-                        regroup_up(0, 0)
                     if it == -3:
                         quantise_up(0, 1)
                     if it == -2:
-                        quantise_up(1, 0)
-                    for j, chunk in todo[len(todo) * 2 // CHUNKS : len(todo) * 3 // CHUNKS]:
-                        run_unit(j, chunk)
+                        regroup_up(2, 0)
+                    if it == -1:
+                        quantise_up(1, 1)
+                    if it == 0:
+                        quantise_up(2, 1)
+                    if it == 1:
+                        quantise_up(3, 1)
+                    run_units(len(todo) * 3 // CHUNKS - len(todo) * 2 // CHUNKS)
                 if c == 3:
-                    collect(it)
+                    transpose(it)
                     if in_range(it + 3):
                         normalise(it + 3)
                     if it == -6:
                         prepare_wo()
+                        wo_q.extend(quantise_weight(wo_grouped[0], "wo"))
                         spread_gain()
                     if it == -4:
-                        quantise_up(0, 0)
                         regroup_up(1, 0)
                     if it == -3:
-                        regroup_up(1, 1)
-                    if it == -2:
-                        regroup_up(2, 0)
-                        quantise_up(1, 1)
-                    if it == -1:
-                        regroup_up(2, 1)
-                    if it == 0:
-                        regroup_up(3, 1)
-                        quantise_up(2, 1)
-                    if it == 1:
-                        quantise_up(3, 1)
-                    for j, chunk in todo[len(todo) * 3 // CHUNKS : len(todo) * 4 // CHUNKS]:
-                        run_unit(j, chunk)
-                if c == 4:
-                    quantise(it)
-                    if it == -5:
-                        regroup_up(0, 1)
+                        quantise_up(1, 0)
                     if it == -1:
                         quantise_up(2, 0)
+                    run_units(len(todo) * 4 // CHUNKS - len(todo) * 3 // CHUNKS)
+                if c == 4:
+                    collect(it)
+                    quantise(it)
+        run_units(len(order) - len(finished))

@@ -175,7 +175,7 @@ def tile_model_pb_kernel(tc, o_attn, xm, attn_o_w, ffn_norm_w, ffn_up_w, out_0, 
             start = X2_PAD + D * (j % PAIR)
             x2 = x2_ring[:, j // PAIR % X2_RING, start : start + D]
             live["x2", j] = x2
-            nc.vector.tensor_tensor(out=x2, in0=acc[:], in1=xm_sb[j], op=ALU.add)
+            nc.vector.tensor_tensor(out=x2, in0=xm_sb[j], in1=acc[:], op=ALU.add)
             if j % PAIR == PAIR - 1:
                 nc.sync.dma_start(
                     out=x2_rows[:, j - 1 : j + 1, :].rearrange("p j d -> p (j d)"),
@@ -193,9 +193,27 @@ def tile_model_pb_kernel(tc, o_attn, xm, attn_o_w, ffn_norm_w, ffn_up_w, out_0, 
             live["rstd", j] = rstd
             nc.gpsimd.tensor_tensor(out=rstd[:], in0=mean_sq[:], in1=neg_half[:], op=ALU.pow)
 
+        def on_gpsimd(j):
+            return j >= 4 and j % 2 == 0
+
+        def apply_gain(j):
+            x2_gain = stage.tile([P, D], F32)
+            live["x2_gain", j] = x2_gain
+            nc.gpsimd.tensor_tensor(out=x2_gain[:], in0=live["x2", j], in1=gain[:], op=ALU.mult)
+
         def normalise(j):
             xn = stage.tile([P, D], BF16)
             live["xn", j] = xn
+            if on_gpsimd(j):
+                nc.gpsimd.tensor_scalar(
+                    out=xn[:],
+                    in0=live["x2_gain", j][:],
+                    scalar1=live["rstd", j][:],
+                    scalar2=1.0,
+                    op0=ALU.mult,
+                    op1=ALU.mult,
+                )
+                return
             nc.vector.scalar_tensor_tensor(
                 out=xn[:], in0=live["x2", j], scalar=live["rstd", j][:], in1=gain[:], op0=ALU.mult, op1=ALU.mult
             )
@@ -269,7 +287,7 @@ def tile_model_pb_kernel(tc, o_attn, xm, attn_o_w, ffn_norm_w, ffn_up_w, out_0, 
             h = h_tiles[j]
             u_ps = pass_of(1, j, first, width)
             nc.vector.tensor_tensor(
-                out=h[:, first : first + width], in0=u_ps[:, :width], in1=live["silu", j, first][:, :width], op=ALU.mult
+                out=h[:, first : first + width], in0=live["silu", j, first][:, :width], in1=u_ps[:, :width], op=ALU.mult
             )
             last = first + width
             if j == TILES - 1:
@@ -336,6 +354,10 @@ def tile_model_pb_kernel(tc, o_attn, xm, attn_o_w, ffn_norm_w, ffn_up_w, out_0, 
                 if c == 1:
                     if in_range(it + 3):
                         mean_square(it + 3)
+                        if on_gpsimd(it + 3):
+                            normalise(it + 3)
+                    if in_range(it + 4) and on_gpsimd(it + 4):
+                        apply_gain(it + 4)
                     if it == -4:
                         quantise_up(0, 0)
                     if it == -3:
@@ -346,6 +368,7 @@ def tile_model_pb_kernel(tc, o_attn, xm, attn_o_w, ffn_norm_w, ffn_up_w, out_0, 
                         regroup_up(3, 0)
                     run_units(len(todo) * 2 // CHUNKS - len(todo) * 1 // CHUNKS)
                 if c == 2:
+                    transpose(it)
                     if it == -3:
                         quantise_up(0, 1)
                     if it == -2:
@@ -358,8 +381,8 @@ def tile_model_pb_kernel(tc, o_attn, xm, attn_o_w, ffn_norm_w, ffn_up_w, out_0, 
                         quantise_up(3, 1)
                     run_units(len(todo) * 3 // CHUNKS - len(todo) * 2 // CHUNKS)
                 if c == 3:
-                    transpose(it)
-                    if in_range(it + 3):
+                    collect(it)
+                    if in_range(it + 3) and not on_gpsimd(it + 3):
                         normalise(it + 3)
                     if it == -6:
                         prepare_wo()
@@ -373,6 +396,5 @@ def tile_model_pb_kernel(tc, o_attn, xm, attn_o_w, ffn_norm_w, ffn_up_w, out_0, 
                         quantise_up(2, 0)
                     run_units(len(todo) * 4 // CHUNKS - len(todo) * 3 // CHUNKS)
                 if c == 4:
-                    collect(it)
                     quantise(it)
         run_units(len(order) - len(finished))

@@ -241,7 +241,8 @@ def tile_model_pb_kernel(tc, o_attn, xm, attn_o_w, ffn_norm_w, ffn_up_w, out_0, 
             k0, k1 = kinds[0], kinds[-1] + 1
             grouped = stage.tile([P, 2, D], BF16, align_bytes=64, name="turned_grouped")
             live["grouped", it] = (grouped, k0, k1)
-            nc.scalar.copy(
+            copy_engine = nc.vector.tensor_copy if on_gpsimd(it + 3) else nc.scalar.copy
+            copy_engine(
                 out=grouped[:, k0:k1, :].bitcast(F32).rearrange("p k (r u) -> p k r u", u=2),
                 in_=turned[:, k0:k1, :, :].rearrange("p k u r -> p k r u"),
             )
@@ -290,10 +291,8 @@ def tile_model_pb_kernel(tc, o_attn, xm, attn_o_w, ffn_norm_w, ffn_up_w, out_0, 
                 out=h[:, first : first + width], in0=live["silu", j, first][:, :width], in1=u_ps[:, :width], op=ALU.mult
             )
             last = first + width
-            if j == TILES - 1:
+            if j >= TILES - 1:
                 store_from = first
-            elif CHUNKS <= j < TILES - 5:
-                store_from = 0 if last == F else last
             else:
                 store_from = last - F // 2 if last % (F // 2) == 0 else last
             if store_from < last:

from contextlib import ExitStack

import concourse.mybir as mybir
from concourse.masks import make_identity

F32 = mybir.dt.float32
BF16 = mybir.dt.bfloat16
U32 = mybir.dt.uint32
U8 = mybir.dt.uint8
FP8X4 = mybir.dt.float8_e4m3fn_x4
ACT = mybir.ActivationFunctionType
ALU = mybir.AluOpType

P = 128
PACK = 4
D = P * PACK
TOKENS = 4 * 576
TILES = TOKENS // P
PAIR = 2
F = 2048
N_PASS = 512
CHUNKS = F // N_PASS
LEAD = 6
EPS = 1e-5
X2_RING = 5
X2_PAD = 8

FLOPS = 2 * TOKENS * D * (D + 2 * F)


def tile_model_pb_kernel(tc, o_attn, xm, attn_o_w, ffn_norm_w, ffn_up_w, out_0, out_1):
    nc = tc.nc

    o_rows = o_attn.flatten_outer_dims().rearrange("(p j) d -> p j d", j=TILES)
    xm_rows = xm.flatten_outer_dims().rearrange("(p j) d -> p j d", j=TILES)
    x2_rows = out_0.flatten_outer_dims().rearrange("(p j) d -> p j d", j=TILES)
    h_rows = out_1.flatten_outer_dims().rearrange("(p j) f -> p j f", j=TILES)

    with ExitStack() as ctx:
        ctx.enter_context(tc.manual_schedule())
        loads = ctx.enter_context(tc.tile_pool(name="loads", bufs=1))
        consts = ctx.enter_context(tc.tile_pool(name="consts", bufs=1))
        weights = ctx.enter_context(tc.tile_pool(name="weights", bufs=1))
        regroup = ctx.enter_context(tc.tile_pool(name="regroup", bufs=4))
        stage = ctx.enter_context(tc.tile_pool(name="stage", bufs=4))
        gated = ctx.enter_context(tc.tile_pool(name="gated", bufs=6))
        results = ctx.enter_context(tc.tile_pool(name="results", bufs=6))
        psum = ctx.enter_context(tc.psum_pool(name="psum", bufs=1))

        gain_row = consts.tile([P, D], BF16)
        nc.vector.memset(gain_row[:], 0.0)
        dummy_in = consts.tile([P, 1], F32)
        nc.vector.memset(dummy_in[:], 0.0)
        dummy_out = consts.tile([P, 1], F32)
        nc.scalar.activation(out=dummy_out[:], in_=dummy_in[:], func=ACT.Silu)
        ident_f32 = consts.tile([P, P], F32)
        make_identity(nc, ident_f32[:])
        ones = consts.tile([P, P], BF16)
        nc.vector.memset(ones[:], 1.0)
        neg_half = consts.tile([P, 1], F32)
        nc.vector.memset(neg_half[:], -0.5)

        groups = ((0, 2), (2, 4), (4, 6), (6, 12), (12, 18))
        o_sb = {}
        xm_sb = {}

        def load_tokens(name, rows, where, g):
            first, last = groups[g]
            group = loads.tile([P, last - first, D], BF16, name="%s%d" % (name, g))
            nc.sync.dma_start(out=group[:], in_=rows[:, first:last, :])
            for j in range(first, last):
                where[j] = group[:, j - first, :]

        def load_o(g):
            load_tokens("o_sb", o_rows, o_sb, g)

        def load_xm(g):
            load_tokens("xm_sb", xm_rows, xm_sb, g)

        wo_rows = attn_o_w.rearrange("(p t) n -> p t n", t=PACK)
        up_rows = ffn_up_w.rearrange("(p t) n -> p t n", t=PACK)
        wo_raw = loads.tile([P, PACK, D], BF16)
        up_raw = [[], []]

        def load_up(first_chunk, chunks):
            for half in range(2):
                raw = loads.tile([P, PACK, chunks * N_PASS], BF16, name="up_raw%d_%d" % (half, first_chunk))
                first = F * half + N_PASS * first_chunk
                nc.sync.dma_start(out=raw[:], in_=up_rows[:, :, first : first + chunks * N_PASS])
                for i in range(chunks):
                    up_raw[half].append(raw[:, :, N_PASS * i : N_PASS * (i + 1)])

        load_o(0)
        nc.sync.dma_start(out=gain_row[0:1, :], in_=ffn_norm_w.unsqueeze(0))
        nc.sync.dma_start(out=wo_raw[:], in_=wo_rows)
        load_xm(0)
        load_up(0, 1)
        load_o(1)
        load_up(1, 1)
        load_xm(1)
        load_o(2)
        load_up(2, 2)
        load_xm(2)
        load_o(3)
        load_xm(3)
        load_o(4)
        load_xm(4)


        def new_grouped():
            grouped = regroup.tile([P, N_PASS, PACK], BF16, tag="grouped", align_bytes=64)
            return grouped

        def regroup_columns(copy_engine, grouped, raw, first, last):
            copy_engine(
                out=grouped[:, first:last, :].rearrange("p (c i) t -> p c t i", i=4),
                in_=raw[:, :, first:last].rearrange("p t (c i) -> p c t i", i=4),
            )

        def quantise_weight(grouped, name):
            codes = weights.tile([P, N_PASS], U32, name=name + "_codes", align_bytes=64)
            scales = weights.tile([P, N_PASS], U8, name=name + "_scales", align_bytes=64)
            nc.vector.quantize_mx(
                out=codes[:].bitcast(FP8X4),
                scales=scales[:],
                in_=grouped[:].rearrange("p w t -> p (w t)"),
            )
            return codes, scales

        wo_q = []
        wo_grouped = []
        up_grouped = {}
        up_q = {}

        def prepare_wo():
            wo_grouped.append(new_grouped())
            regroup_columns(nc.vector.tensor_copy, wo_grouped[0], wo_raw, 0, 352)
            regroup_columns(nc.scalar.copy, wo_grouped[0], wo_raw, 352, N_PASS)

        def regroup_up(c, half):
            up_grouped[half, c] = new_grouped()
            if half:
                regroup_columns(nc.scalar.copy, up_grouped[half, c], up_raw[half][c], 0, N_PASS)
            else:
                regroup_columns(nc.vector.tensor_copy, up_grouped[half, c], up_raw[half][c], 0, N_PASS)

        def quantise_up(c, half):
            up_q[half, c] = quantise_weight(up_grouped[half, c], "up%d_%d" % (half, c))

        live = {}

        x2_ring = consts.tile([P, X2_RING, PAIR * D + 2 * X2_PAD], F32)
        for column in (X2_PAD - 1, X2_PAD + PAIR * D):
            nc.vector.memset(x2_ring[:, :, column : column + 1], (D * EPS) ** 0.5)

        def in_range(j):
            return 0 <= j < TILES

        def project(j):
            codes, scales, cols = live["o", j]
            acc = psum.tile([P, D], F32, tag="acc")
            nc.tensor.matmul_mx(
                out=acc[:],
                lhsT=codes[:, cols].bitcast(FP8X4),
                lhsT_scale=scales[:, cols],
                rhs=wo_q[0][:].bitcast(FP8X4),
                rhs_scale=wo_q[1][:],
                start=True,
                stop=True,
            )
            live["acc", j] = acc

        def residual(j):
            acc = live["acc", j]
            start = X2_PAD + D * (j % PAIR)
            x2 = x2_ring[:, j // PAIR % X2_RING, start : start + D]
            live["x2", j] = x2
            nc.vector.tensor_tensor(out=x2, in0=xm_sb[j], in1=acc[:], op=ALU.add)
            if j % PAIR == PAIR - 1:
                nc.sync.dma_start(
                    out=x2_rows[:, j - 1 : j + 1, :].rearrange("p j d -> p (j d)"),
                    in_=x2_ring[:, j // PAIR % X2_RING, X2_PAD : X2_PAD + PAIR * D],
                )

        def mean_square(j):
            squares = stage.tile([P, D + 1], BF16)
            mean_sq = stage.tile([P, 1], F32)
            start = X2_PAD - 1 if j % PAIR == 0 else X2_PAD + D
            nc.scalar.activation(
                out=squares[:], in_=x2_ring[:, j // PAIR % X2_RING, start : start + D + 1], func=ACT.Square, scale=D**-0.5, accum_out=mean_sq[:]
            )
            rstd = stage.tile([P, 1], F32)
            live["rstd", j] = rstd
            nc.gpsimd.tensor_tensor(out=rstd[:], in0=mean_sq[:], in1=neg_half[:], op=ALU.pow)

        def on_gpsimd(j):
            return j >= 4 and j % 2 == 0

        def apply_gain(j):
            x2_gain = stage.tile([P, D], F32)
            live["x2_gain", j] = x2_gain
            nc.gpsimd.tensor_tensor(out=x2_gain[:], in0=live["x2", j], in1=gain[:], op=ALU.mult)

        def normalise(j):
            xn = stage.tile([P, D], BF16)
            live["xn", j] = xn
            if on_gpsimd(j):
                nc.gpsimd.tensor_scalar(
                    out=xn[:],
                    in0=live["x2_gain", j][:],
                    scalar1=live["rstd", j][:],
                    scalar2=1.0,
                    op0=ALU.mult,
                    op1=ALU.mult,
                )
                return
            nc.vector.scalar_tensor_tensor(
                out=xn[:], in0=live["x2", j], scalar=live["rstd", j][:], in1=gain[:], op0=ALU.mult, op1=ALU.mult
            )

        def transpose(it):
            ja, je = it + 6, it + 2
            kinds = []
            turned = psum.tile([P, 2, 2, P], F32)
            if in_range(ja):
                words = o_sb[ja].bitcast(F32)
                for u in range(2):
                    nc.tensor.transpose(turned[:, 0, u, :], words[:, u : D // 2 : 2], ident_f32[:])
                kinds.append(0)
            if in_range(je):
                words = live["xn", je][:].bitcast(F32)
                for u in range(2):
                    nc.tensor.transpose(turned[:, 1, u, :], words[:, u : D // 2 : 2], ident_f32[:])
                kinds.append(1)
            live["turned", it] = (turned, kinds)

        def collect(it):
            turned, kinds = live["turned", it]
            if not kinds:
                return
            k0, k1 = kinds[0], kinds[-1] + 1
            grouped = stage.tile([P, 2, D], BF16, align_bytes=64, name="turned_grouped")
            live["grouped", it] = (grouped, k0, k1)
            copy_engine = nc.vector.tensor_copy if on_gpsimd(it + 3) else nc.scalar.copy
            copy_engine(
                out=grouped[:, k0:k1, :].bitcast(F32).rearrange("p k (r u) -> p k r u", u=2),
                in_=turned[:, k0:k1, :, :].rearrange("p k u r -> p k r u"),
            )

        def quantise(it):
            if ("grouped", it) not in live:
                return
            grouped, k0, k1 = live["grouped", it]
            codes = stage.tile([P, 2 * P], U32, align_bytes=64, bufs=6)
            scales = stage.tile([P, 2 * P], U8, align_bytes=64, bufs=6)
            nc.vector.quantize_mx(
                out=codes[:, P * k0 : P * k1].bitcast(FP8X4),
                scales=scales[:, P * k0 : P * k1],
                in_=grouped[:, k0:k1, :].rearrange("p k d -> p (k d)"),
            )
            live["o", it + 6] = (codes, scales, slice(0, P))
            live["xn_q", it + 2] = (codes, scales, slice(P, 2 * P))

        def pass_of(half, j, first, width):
            codes, scales, cols = live["xn_q", j]
            c, offset = divmod(first, N_PASS)
            u_ps = psum.tile([P, N_PASS], F32, name="u%d" % half, bufs=3)
            nc.tensor.matmul_mx(
                out=u_ps[:, :width],
                lhsT=codes[:, cols].bitcast(FP8X4),
                lhsT_scale=scales[:, cols],
                rhs=up_q[half, c][0][:, offset : offset + width].bitcast(FP8X4),
                rhs_scale=up_q[half, c][1][:, offset : offset + width],
                start=True,
                stop=True,
            )
            return u_ps

        def start_unit(j, first, width):
            silu = gated.tile([P, N_PASS], F32)
            live["silu", j, first] = silu
            u_ps = pass_of(0, j, first, width)
            nc.scalar.activation(out=silu[:, :width], in_=u_ps[:, :width], func=ACT.Silu)

        def finish_unit(j, first, width):
            if first == 0:
                h_tiles[j] = results.tile([P, F], F32, name="h")
            h = h_tiles[j]
            u_ps = pass_of(1, j, first, width)
            nc.vector.tensor_tensor(
                out=h[:, first : first + width], in0=live["silu", j, first][:, :width], in1=u_ps[:, :width], op=ALU.mult
            )
            last = first + width
            if j >= TILES - 1:
                store_from = first
            else:
                store_from = last - F // 2 if last % (F // 2) == 0 else last
            if store_from < last:
                nc.sync.dma_start(out=h_rows[:, j, store_from:last], in_=h[:, store_from:last])

        gain = consts.tile([P, D], F32)

        def spread_gain():
            gain_ps = psum.tile([P, D], F32, tag="acc")
            nc.tensor.matmul(out=gain_ps[:], lhsT=ones[:], rhs=gain_row[:], start=True, stop=True)
            nc.vector.tensor_copy(out=gain[:], in_=gain_ps[:])

        h_tiles = {}

        def units(it):
            if it < 0:
                return []
            if it < CHUNKS:
                return [(it, c) for c in range(it)] + [(j, it) for j in range(it + 1)]
            return [(it, c) for c in range(CHUNKS)]

        order = []
        for it in range(TILES):
            for j, c in units(it):
                pieces = 2 if (j, c) == (TILES - 1, CHUNKS - 1) else 1
                width = N_PASS // pieces
                order.extend((j, N_PASS * c + width * i, width) for i in range(pieces))
        started = []
        finished = []

        def run_units(count):
            for k in range(count):
                ahead = len(finished) + 1
                while len(started) < min(ahead + 1, len(order)):
                    unit = order[len(started)]
                    start_unit(unit[0], unit[1], unit[2])
                    started.append(unit)
                unit = order[len(finished)]
                finish_unit(unit[0], unit[1], unit[2])
                finished.append(unit)

        for it in range(-LEAD, TILES):
            todo = units(it)
            for c in range(CHUNKS + 1):
                if c == 0:
                    if in_range(it + 4):
                        project(it + 4)
                    if in_range(it + 4):
                        residual(it + 4)
                    if it == -5:
                        regroup_up(0, 0)
                    if it == -4:
                        regroup_up(0, 1)
                    if it == 1:
                        quantise_up(3, 0)
                        regroup_up(3, 1)
                    run_units(len(todo) * 1 // CHUNKS - len(todo) * 0 // CHUNKS)
                if c == 1:
                    if in_range(it + 3):
                        mean_square(it + 3)
                        if on_gpsimd(it + 3):
                            normalise(it + 3)
                    if in_range(it + 4) and on_gpsimd(it + 4):
                        apply_gain(it + 4)
                    if it == -4:
                        quantise_up(0, 0)
                    if it == -3:
                        regroup_up(1, 1)
                    if it == -1:
                        regroup_up(2, 1)
                    if it == 0:
                        regroup_up(3, 0)
                    run_units(len(todo) * 2 // CHUNKS - len(todo) * 1 // CHUNKS)
                if c == 2:
                    transpose(it)
                    if it == -3:
                        quantise_up(0, 1)
                    if it == -2:
                        regroup_up(2, 0)
                    if it == -1:
                        quantise_up(1, 1)
                    if it == 0:
                        quantise_up(2, 1)
                    if it == 1:
                        quantise_up(3, 1)
                    run_units(len(todo) * 3 // CHUNKS - len(todo) * 2 // CHUNKS)
                if c == 3:
                    collect(it)
                    if in_range(it + 3) and not on_gpsimd(it + 3):
                        normalise(it + 3)
                    if it == -6:
                        prepare_wo()
                        wo_q.extend(quantise_weight(wo_grouped[0], "wo"))
                        spread_gain()
                    if it == -4:
                        regroup_up(1, 0)
                    if it == -3:
                        quantise_up(1, 0)
                    if it == -1:
                        quantise_up(2, 0)
                    run_units(len(todo) * 4 // CHUNKS - len(todo) * 3 // CHUNKS)
                if c == 4:
                    quantise(it)
        run_units(len(order) - len(finished))
